import numpy as np
import ml_dtypes


def mxq(x, axis, fmt="e4m3"):
    dtype, down = {"e4m3": (ml_dtypes.float8_e4m3fn, 7), "e5m2": (ml_dtypes.float8_e5m2, 14)}[fmt]
    v = np.moveaxis(np.asarray(x, np.float32).astype(ml_dtypes.bfloat16).astype(np.float64), axis, -1)
    blocks = v.reshape(v.shape[:-1] + (-1, 32))
    amax = np.abs(blocks).max(-1, keepdims=True)
    byte = np.maximum(np.where(amax > 0, np.frexp(amax)[1] - 1 + 127, 0) - down, 1)
    scale = np.exp2(byte - 127.0)
    codes = (blocks / scale).astype(np.float32).astype(dtype).astype(np.float64)
    return np.moveaxis((codes * scale).reshape(v.shape), -1, axis)


WIDE = False


def mx_kscale(k):
    if not WIDE:
        return np.ones(k)
    levels = np.array([10, -10, 5, -5, 0])
    if k % 512:
        return np.exp2(np.random.permutation(np.resize(levels, k // 32))).repeat(32)
    a = np.empty((k // 512, 16))
    for p in range(k // 512):
        a[p, :8] = np.random.permutation(np.resize(levels, 8))
        for g in range(8):
            far = levels[np.abs(levels - a[p, g]) >= 10]
            a[p, g + 8] = far[np.random.randint(len(far))]
    return np.exp2(a.ravel()).repeat(32)


BF16 = ml_dtypes.bfloat16


def bf(x):
    return np.asarray(x, np.float32).astype(BF16)


def f64(x):
    return np.asarray(x).astype(np.float64)


I, H, B = 2048, 2048, 128


def sigmoid(v):
    return 1.0 / (1.0 + np.exp(-v))


def setup_inputs():
    s, t = mx_kscale(I), mx_kscale(H)
    d = {"x": bf(np.random.standard_normal((I, B)) * s[:, None]), "h": bf(np.random.standard_normal((B, H)) * t[None, :])}
    for n in ("w_ii", "w_ig"):
        d[n] = bf(np.random.standard_normal((H, I)) * 0.7 / np.sqrt(I) / s[None, :])
    for n in ("w_hi", "w_hg"):
        d[n] = bf(np.random.standard_normal((H, H)) * 0.7 / np.sqrt(H) / t[None, :])
    for n in ("b_ii", "b_hi", "b_ig", "b_hg"):
        d[n] = bf(np.random.standard_normal((H, 1)) * 0.3)
    return d


def reference(x, h, w_ii, w_ig, w_hi, w_hg, b_ii, b_hi, b_ig, b_hg):
    xq = mxq(f64(x), 0, "e4m3")
    hq = mxq(f64(h).T, 0, "e4m3")
    i = sigmoid((mxq(f64(w_ii), 1, "e4m3") @ xq) + f64(b_ii) + (mxq(f64(w_hi), 1, "e4m3") @ hq) + f64(b_hi))
    g = np.tanh((mxq(f64(w_ig), 1, "e4m3") @ xq) + f64(b_ig) + (mxq(f64(w_hg), 1, "e4m3") @ hq) + f64(b_hg))
    return i * g

@@ -1,0 +1,231 @@
+from contextlib import ExitStack
+
+import concourse.mybir as mybir
+from concourse.masks import make_identity
+
+F32 = mybir.dt.float32
+BF16 = mybir.dt.bfloat16
+U32 = mybir.dt.uint32
+U8 = mybir.dt.uint8
+FP8X4 = mybir.dt.float8_e4m3fn_x4
+ACT = mybir.ActivationFunctionType
+ALU = mybir.AluOpType
+
+P = 128
+K = 2048
+NT = 16
+B = 128
+FLOPS = 2 * 4 * 2048 * 2048 * 128
+
+PAIRS = 7
+LAG_PASSES = 8
+TAIL_STEPS = 4
+NB = 12
+T_BANKS = 6
+ACC_BANKS = 2
+GRP_BUFS = 6
+CODE_BUFS = 14
+
+
+def tile_naivelstm_pa_kernel(tc, x, h, w_ii, w_ig, w_hi, w_hg, b_ii, b_hi, b_ig, b_hg, out):
+    nc = tc.nc
+    with ExitStack() as ctx:
+        ctx.enter_context(tc.manual_schedule())
+        const = ctx.enter_context(tc.tile_pool(name="const", bufs=1))
+        rawp = ctx.enter_context(tc.tile_pool(name="rawp", bufs=NB))
+        grpp = ctx.enter_context(tc.tile_pool(name="grpp", bufs=GRP_BUFS))
+        codp = ctx.enter_context(tc.tile_pool(name="codp", bufs=CODE_BUFS))
+        tps = ctx.enter_context(tc.psum_pool(name="tps", bufs=T_BANKS))
+        accp = ctx.enter_context(tc.psum_pool(name="accp", bufs=ACC_BANKS))
+
+        weights = {("i", "x"): w_ii, ("i", "h"): w_hi, ("g", "x"): w_ig, ("g", "h"): w_hg}
+        out_v = out.rearrange("(p t) b -> p t b", t=NT)
+
+        stream = []
+        for pair in range(PAIRS):
+            for gate in "ig":
+                for half in "xh":
+                    stream.append((gate, half, 2 * pair, 2, 0, 4))
+        for gate in "ig":
+            for t in range(2 * PAIRS, NT):
+                for half in "xh":
+                    stream.append((gate, half, t, 1, 0, 4))
+        stream.pop()
+        stream.append(("g", "h", NT - 1, 1, 0, 2))
+        stream.append(("g", "h", NT - 1, 1, 2, 2))
+        n_steps = len(stream)
+
+        raw_tiles = {}
+
+        def load(ci):
+            gate, half, t0, n, g0, ng = stream[ci]
+            rt = rawp.tile([P, 2 * K], BF16, name="wraw", tag="wraw")
+            src = weights[(gate, half)].rearrange("(p t) k -> p t k", t=NT)[:, t0 : t0 + n, 512 * g0 : 512 * (g0 + ng)]
+            nc.sync.dma_start(out=rt[:, : n * ng * 512].rearrange("p (t k) -> p t k", t=n), in_=src)
+            raw_tiles[ci] = rt
+
+        group_units = {}
+        for ci in range(n_steps):
+            gate, half, t0, n, g0, ng = stream[ci]
+            for j in range(n):
+                group_units[(gate, t0 + j)] = group_units.get((gate, t0 + j), []) + [(ci, j)]
+        sets = []
+        for pair in range(NT // 2):
+            for gate in "ig":
+                if pair < PAIRS:
+                    sets.append([(gate, 2 * pair)])
+                    sets.append([(gate, 2 * pair + 1)])
+        for gate in "ig":
+            for t in range(2 * PAIRS, NT):
+                sets.append([(gate, t)])
+        runs = {}
+        for st in sets:
+            place = max([group_units[grp][-1][0] for grp in st])
+            ahead = 0
+            while place < n_steps - 1 and ahead < LAG_PASSES:
+                place += 1
+                ahead += stream[place][3] * stream[place][5]
+            if st[0][1] < 2 * PAIRS and st[0][1] % 2 == 1:
+                place += 1
+            if place >= n_steps - TAIL_STEPS:
+                place = n_steps - 1
+            runs[place] = runs.get(place, []) + [st]
+
+        ident = const.tile([P, P], F32, name="ident")
+        make_identity(nc, ident[:])
+
+        braw = {}
+        for nm, ap in (("ii", b_ii), ("hi", b_hi), ("ig", b_ig), ("hg", b_hg)):
+            bt = const.tile([P, NT], BF16, name="braw_" + nm)
+            nc.scalar.dma_start(out=bt[:], in_=ap.rearrange("(p t) o -> p (t o)", t=NT))
+            braw[nm] = bt
+
+        hraw = const.tile([P, K], BF16, name="hraw")
+        nc.sync.dma_start(out=hraw[:], in_=h)
+        xraw = const.tile([P, 4, 512], BF16, name="xraw")
+        nc.sync.dma_start(out=xraw[:], in_=x.rearrange("(g p t) c -> p g (t c)", g=4, p=P, t=4))
+        for ci in range(NB):
+            load(ci)
+
+        warm = const.tile([P, 1], F32, name="warm")
+        nc.vector.memset(warm[:], 0.0)
+        warm2 = const.tile([P, 1], F32, name="warm2")
+        nc.scalar.activation(out=warm2[:], in_=warm[:], func=ACT.Sigmoid)
+
+        gate_out = {}
+        for gate in "ig":
+            gate_out[gate] = const.tile([P, NT, B], F32, name="gate_" + gate)
+        osb = const.tile([P, NT, B], F32, name="osb")
+
+        def transposes(src_words, ng):
+            banks = []
+            for b in range(ng // 2):
+                tb = tps.tile([P, 4, P], F32, name="tb", tag="tb")
+                for q in range(4):
+                    w0 = (4 * b + 2 * (q // 2)) * P
+                    nc.tensor.transpose(tb[:, q, :], src_words[:, w0 + q % 2 : w0 + 2 * P : 2], ident[:])
+                banks.append(tb)
+            return banks
+
+        def copy_bank(eng, grp, b, tb):
+            dst = grp[:].bitcast(F32)[:, 512 * b : 512 * (b + 1)].rearrange("p (g r u) -> p g r u", g=2, u=2)
+            src = tb[:].rearrange("p (g u) r -> p g r u", u=2)
+            if eng == "s":
+                nc.scalar.copy(out=dst, in_=src)
+            else:
+                nc.vector.tensor_copy(out=dst, in_=src)
+
+        def quantise(grp, codes, scl, ng):
+            nc.vector.quantize_mx(
+                out=codes[:, : P * ng].bitcast(FP8X4), scales=scl[:, : P * ng], in_=grp[:, : 512 * ng]
+            )
+
+        hb = transposes(hraw[:].bitcast(F32), 4)
+        hgrp = grpp.tile([P, K], BF16, name="grp", tag="grp", align_bytes=64)
+        copy_bank("s", hgrp, 0, hb[0])
+        copy_bank("v", hgrp, 1, hb[1])
+        xgrp = grpp.tile([P, K], BF16, name="grp", tag="grp", align_bytes=64)
+        nc.vector.tensor_copy(
+            out=xgrp[:].rearrange("p (g c j) -> p g c j", g=4, j=4),
+            in_=xraw[:].rearrange("p a b -> p (a b)").rearrange("p (g j c) -> p g c j", g=4, j=4),
+        )
+        act_codes = {}
+        act_scales = {}
+        for nm, grp in (("h", hgrp), ("x", xgrp)):
+            ac = const.tile([P, 512], U32, name="actc_" + nm, align_bytes=64)
+            asc = const.tile([P, 512], U8, name="acts_" + nm, align_bytes=64)
+            quantise(grp, ac, asc, 4)
+            act_codes[nm] = ac
+            act_scales[nm] = asc
+
+        bias = {}
+        for gate, n0, n1 in (("i", "ii", "hi"), ("g", "ig", "hg")):
+            bs = const.tile([P, NT], F32, name="bias_" + gate)
+            nc.vector.tensor_tensor(out=bs[:], in0=braw[n0][:], in1=braw[n1][:], op=ALU.add)
+            bias[gate] = bs
+
+        unit_codes = {}
+
+        def mx_set(st):
+            acc = accp.tile([P, 2, B], F32, name="acc", tag="acc")
+            for si, grp in enumerate(st):
+                passes = []
+                for ci, j in group_units[grp]:
+                    for gl in range(stream[ci][5]):
+                        passes.append((ci, j, gl))
+                for pi, (ci, j, gl) in enumerate(passes):
+                    half = stream[ci][1]
+                    g = stream[ci][4] + gl
+                    codes, scl = unit_codes[(ci, j)]
+                    nc.tensor.matmul_mx(
+                        out=acc[:, si, :],
+                        lhsT=codes[:, P * gl : P * (gl + 1)].bitcast(FP8X4),
+                        lhsT_scale=scl[:, P * gl : P * (gl + 1)],
+                        rhs=act_codes[half][:, P * g : P * (g + 1)].bitcast(FP8X4),
+                        rhs_scale=act_scales[half][:, P * g : P * (g + 1)],
+                        start=(pi == 0),
+                        stop=(pi == len(passes) - 1),
+                    )
+            gate = st[0][0]
+            for si, (gt, t) in enumerate(st):
+                nc.scalar.activation(
+                    out=gate_out[gate][:, t, :],
+                    in_=acc[:, si, :],
+                    func=(ACT.Sigmoid if gate == "i" else ACT.Tanh),
+                    bias=bias[gate][:, t : t + 1],
+                    scale=1.0,
+                )
+            hi = st[-1][1] + 1
+            lo = hi - 1 if hi > 2 * PAIRS else hi - 2
+            if gate == "g" and (hi > 2 * PAIRS or hi % 2 == 0):
+                nc.vector.tensor_tensor(
+                    out=osb[:, lo:hi, :], in0=gate_out["i"][:, lo:hi, :], in1=gate_out["g"][:, lo:hi, :], op=ALU.mult
+                )
+                if hi == 2 * PAIRS:
+                    nc.sync.dma_start(out=out_v[:, 0:hi, :], in_=osb[:, 0:hi, :])
+                elif hi > 2 * PAIRS:
+                    nc.sync.dma_start(out=out_v[:, lo:hi, :], in_=osb[:, lo:hi, :])
+
+        bank_count = 0
+        for ci in range(n_steps):
+            gate, half, t0, n, g0, ng = stream[ci]
+            words = raw_tiles[ci][:].bitcast(F32)
+            banks = []
+            for j in range(n):
+                banks.append(transposes(words[:, j * 256 * ng : (j + 1) * 256 * ng], ng))
+            if ci + NB < n_steps:
+                load(ci + NB)
+            grps = []
+            for j in range(n):
+                grp = grpp.tile([P, K], BF16, name="grp", tag="grp", align_bytes=64)
+                grps.append(grp)
+                for b, tb in enumerate(banks[j]):
+                    bank_count += 1
+                    copy_bank("v" if (ng == 4 and bank_count % 4 == 0) else "s", grp, b, tb)
+            for j in range(n):
+                codes = codp.tile([P, 512], U32, name="codes", tag="codes", align_bytes=64)
+                scl = codp.tile([P, 512], U8, name="scl", tag="scl", align_bytes=64)
+                quantise(grps[j], codes, scl, ng)
+                unit_codes[(ci, j)] = (codes, scl)
+            for st in runs.get(ci, []):
+                mx_set(st)

@@ -20,11 +20,13 @@ FLOPS = 2 * 4 * 2048 * 2048 * 128
 PAIRS = 7
 LAG_PASSES = 8
 TAIL_STEPS = 4
-NB = 12
+NB = 10
 T_BANKS = 6
 ACC_BANKS = 2
 GRP_BUFS = 6
 CODE_BUFS = 14
+ORD_BUFS = 4
+AHEAD = 2
 
 
 def tile_naivelstm_pa_kernel(tc, x, h, w_ii, w_ig, w_hi, w_hg, b_ii, b_hi, b_ig, b_hg, out):
@@ -34,6 +36,7 @@ def tile_naivelstm_pa_kernel(tc, x, h, w_ii, w_ig, w_hi, w_hg, b_ii, b_hi, b_ig,
         const = ctx.enter_context(tc.tile_pool(name="const", bufs=1))
         rawp = ctx.enter_context(tc.tile_pool(name="rawp", bufs=NB))
         grpp = ctx.enter_context(tc.tile_pool(name="grpp", bufs=GRP_BUFS))
+        ordp = ctx.enter_context(tc.tile_pool(name="ordp", bufs=ORD_BUFS))
         codp = ctx.enter_context(tc.tile_pool(name="codp", bufs=CODE_BUFS))
         tps = ctx.enter_context(tc.psum_pool(name="tps", bufs=T_BANKS))
         accp = ctx.enter_context(tc.psum_pool(name="accp", bufs=ACC_BANKS))
@@ -54,6 +57,7 @@ def tile_naivelstm_pa_kernel(tc, x, h, w_ii, w_ig, w_hi, w_hg, b_ii, b_hi, b_ig,
         stream.append(("g", "h", NT - 1, 1, 0, 2))
         stream.append(("g", "h", NT - 1, 1, 2, 2))
         n_steps = len(stream)
+        ordered = [1 <= ci < n_steps - 4 for ci in range(n_steps)]
 
         raw_tiles = {}
 
@@ -117,13 +121,18 @@ def tile_naivelstm_pa_kernel(tc, x, h, w_ii, w_ig, w_hi, w_hg, b_ii, b_hi, b_ig,
             gate_out[gate] = const.tile([P, NT, B], F32, name="gate_" + gate)
         osb = const.tile([P, NT, B], F32, name="osb")
 
-        def transposes(src_words, ng):
+        def transposes(src_words, ng, in_order=False):
             banks = []
             for b in range(ng // 2):
                 tb = tps.tile([P, 4, P], F32, name="tb", tag="tb")
                 for q in range(4):
-                    w0 = (4 * b + 2 * (q // 2)) * P
-                    nc.tensor.transpose(tb[:, q, :], src_words[:, w0 + q % 2 : w0 + 2 * P : 2], ident[:])
+                    if in_order:
+                        w0 = (4 * b + q) * P
+                        words = src_words[:, w0 : w0 + P]
+                    else:
+                        w0 = (4 * b + 2 * (q // 2)) * P
+                        words = src_words[:, w0 + q % 2 : w0 + 2 * P : 2]
+                    nc.tensor.transpose(tb[:, q, :], words, ident[:])
                 banks.append(tb)
             return banks
 
@@ -206,23 +215,51 @@ def tile_naivelstm_pa_kernel(tc, x, h, w_ii, w_ig, w_hi, w_hg, b_ii, b_hi, b_ig,
                 elif hi > 2 * PAIRS:
                     nc.sync.dma_start(out=out_v[:, lo:hi, :], in_=osb[:, lo:hi, :])
 
+        ord_tiles = {}
+
+        def put_in_order(ci, j):
+            ng = stream[ci][5]
+            if ci not in ord_tiles:
+                ot = ordp.tile([P, 2 * K], BF16, name="ordw", tag="ordw")
+                ord_tiles[ci] = ot
+            lo, hi = j * 256 * ng, (j + 1) * 256 * ng
+            nc.vector.tensor_copy(
+                out=ord_tiles[ci][:].bitcast(F32)[:, lo:hi].rearrange("p (g u c) -> p g u c", g=ng, u=2),
+                in_=raw_tiles[ci][:].bitcast(F32)[:, lo:hi].rearrange("p (g c u) -> p g u c", g=ng, u=2),
+            )
+
+        loaded = [NB]
+
+        def next_load():
+            if loaded[0] < n_steps:
+                load(loaded[0])
+                loaded[0] += 1
+
+        for ci in range(AHEAD):
+            if ordered[ci]:
+                for j in range(stream[ci][3]):
+                    put_in_order(ci, j)
         bank_count = 0
         for ci in range(n_steps):
             gate, half, t0, n, g0, ng = stream[ci]
-            words = raw_tiles[ci][:].bitcast(F32)
+            words = (ord_tiles[ci] if ordered[ci] else raw_tiles[ci])[:].bitcast(F32)
             banks = []
             for j in range(n):
-                banks.append(transposes(words[:, j * 256 * ng : (j + 1) * 256 * ng], ng))
-            if ci + NB < n_steps:
-                load(ci + NB)
+                banks.append(transposes(words[:, j * 256 * ng : (j + 1) * 256 * ng], ng, ordered[ci]))
+            next_load()
             grps = []
             for j in range(n):
                 grp = grpp.tile([P, K], BF16, name="grp", tag="grp", align_bytes=64)
                 grps.append(grp)
                 for b, tb in enumerate(banks[j]):
                     bank_count += 1
-                    copy_bank("v" if (ng == 4 and bank_count % 4 == 0) else "s", grp, b, tb)
+                    copy_bank("v" if (ng == 4 and not ordered[ci] and bank_count % 4 == 0) else "s", grp, b, tb)
+            pre = ci + AHEAD
             for j in range(n):
+                if pre < n_steps and ordered[pre]:
+                    for jj in range(stream[pre][3]):
+                        if jj % n == j:
+                            put_in_order(pre, jj)
                 codes = codp.tile([P, 512], U32, name="codes", tag="codes", align_bytes=64)
                 scl = codp.tile([P, 512], U8, name="scl", tag="scl", align_bytes=64)
                 quantise(grps[j], codes, scl, ng)

@@ -18,14 +18,15 @@ B = 128
 FLOPS = 2 * 4 * 2048 * 2048 * 128
 
 PAIRS = 7
-LAG_PASSES = 8
+LAG_PASSES = 16
 TAIL_STEPS = 4
 NB = 10
 T_BANKS = 6
 ACC_BANKS = 2
-GRP_BUFS = 6
-CODE_BUFS = 14
-ORD_BUFS = 4
+GRP_BUFS = 3
+CODE_BUFS = 7
+ORD_BUFS = 3
+FIRST = 2
 AHEAD = 2
 
 
@@ -35,8 +36,8 @@ def tile_naivelstm_pa_kernel(tc, x, h, w_ii, w_ig, w_hi, w_hg, b_ii, b_hi, b_ig,
         ctx.enter_context(tc.manual_schedule())
         const = ctx.enter_context(tc.tile_pool(name="const", bufs=1))
         rawp = ctx.enter_context(tc.tile_pool(name="rawp", bufs=NB))
-        grpp = ctx.enter_context(tc.tile_pool(name="grpp", bufs=GRP_BUFS))
         ordp = ctx.enter_context(tc.tile_pool(name="ordp", bufs=ORD_BUFS))
+        grpp = ctx.enter_context(tc.tile_pool(name="grpp", bufs=GRP_BUFS))
         codp = ctx.enter_context(tc.tile_pool(name="codp", bufs=CODE_BUFS))
         tps = ctx.enter_context(tc.psum_pool(name="tps", bufs=T_BANKS))
         accp = ctx.enter_context(tc.psum_pool(name="accp", bufs=ACC_BANKS))
@@ -57,7 +58,7 @@ def tile_naivelstm_pa_kernel(tc, x, h, w_ii, w_ig, w_hi, w_hg, b_ii, b_hi, b_ig,
         stream.append(("g", "h", NT - 1, 1, 0, 2))
         stream.append(("g", "h", NT - 1, 1, 2, 2))
         n_steps = len(stream)
-        ordered = [1 <= ci < n_steps - 4 for ci in range(n_steps)]
+        ordered = [4 <= ci < n_steps - 3 and ci % 2 == 1 for ci in range(n_steps)]
 
         raw_tiles = {}
 
@@ -65,7 +66,11 @@ def tile_naivelstm_pa_kernel(tc, x, h, w_ii, w_ig, w_hi, w_hg, b_ii, b_hi, b_ig,
             gate, half, t0, n, g0, ng = stream[ci]
             rt = rawp.tile([P, 2 * K], BF16, name="wraw", tag="wraw")
             src = weights[(gate, half)].rearrange("(p t) k -> p t k", t=NT)[:, t0 : t0 + n, 512 * g0 : 512 * (g0 + ng)]
-            nc.sync.dma_start(out=rt[:, : n * ng * 512].rearrange("p (t k) -> p t k", t=n), in_=src)
+            if ci == 0:
+                for j in range(n):
+                    nc.sync.dma_start(out=rt[:, j * K : (j + 1) * K], in_=src[:, j, :])
+            else:
+                nc.sync.dma_start(out=rt[:, : n * ng * 512].rearrange("p (t k) -> p t k", t=n), in_=src)
             raw_tiles[ci] = rt
 
         group_units = {}
@@ -74,26 +79,22 @@ def tile_naivelstm_pa_kernel(tc, x, h, w_ii, w_ig, w_hi, w_hg, b_ii, b_hi, b_ig,
             for j in range(n):
                 group_units[(gate, t0 + j)] = group_units.get((gate, t0 + j), []) + [(ci, j)]
         sets = []
-        for pair in range(NT // 2):
+        for pair in range(PAIRS):
             for gate in "ig":
-                if pair < PAIRS:
-                    sets.append([(gate, 2 * pair)])
-                    sets.append([(gate, 2 * pair + 1)])
+                sets.append([(gate, 2 * pair), (gate, 2 * pair + 1)])
         for gate in "ig":
             for t in range(2 * PAIRS, NT):
                 sets.append([(gate, t)])
         runs = {}
-        for st in sets:
-            place = max([group_units[grp][-1][0] for grp in st])
+        for groups in sets:
+            place = group_units[groups[-1]][-1][0]
             ahead = 0
             while place < n_steps - 1 and ahead < LAG_PASSES:
                 place += 1
                 ahead += stream[place][3] * stream[place][5]
-            if st[0][1] < 2 * PAIRS and st[0][1] % 2 == 1:
-                place += 1
             if place >= n_steps - TAIL_STEPS:
                 place = n_steps - 1
-            runs[place] = runs.get(place, []) + [st]
+            runs[place] = runs.get(place, []) + [groups]
 
         ident = const.tile([P, P], F32, name="ident")
         make_identity(nc, ident[:])
@@ -104,11 +105,13 @@ def tile_naivelstm_pa_kernel(tc, x, h, w_ii, w_ig, w_hi, w_hg, b_ii, b_hi, b_ig,
             nc.scalar.dma_start(out=bt[:], in_=ap.rearrange("(p t) o -> p (t o)", t=NT))
             braw[nm] = bt
 
+        for ci in range(FIRST):
+            load(ci)
         hraw = const.tile([P, K], BF16, name="hraw")
         nc.sync.dma_start(out=hraw[:], in_=h)
         xraw = const.tile([P, 4, 512], BF16, name="xraw")
         nc.sync.dma_start(out=xraw[:], in_=x.rearrange("(g p t) c -> p g (t c)", g=4, p=P, t=4))
-        for ci in range(NB):
+        for ci in range(FIRST, NB):
             load(ci)
 
         warm = const.tile([P, 1], F32, name="warm")
@@ -121,82 +124,80 @@ def tile_naivelstm_pa_kernel(tc, x, h, w_ii, w_ig, w_hi, w_hg, b_ii, b_hi, b_ig,
             gate_out[gate] = const.tile([P, NT, B], F32, name="gate_" + gate)
         osb = const.tile([P, NT, B], F32, name="osb")
 
-        def transposes(src_words, ng, in_order=False):
+        def transposes(words, ng, in_order):
             banks = []
             for b in range(ng // 2):
                 tb = tps.tile([P, 4, P], F32, name="tb", tag="tb")
                 for q in range(4):
-                    if in_order:
-                        w0 = (4 * b + q) * P
-                        words = src_words[:, w0 : w0 + P]
-                    else:
-                        w0 = (4 * b + 2 * (q // 2)) * P
-                        words = src_words[:, w0 + q % 2 : w0 + 2 * P : 2]
-                    nc.tensor.transpose(tb[:, q, :], words, ident[:])
+                    g, u = 2 * b + q // 2, q % 2
+                    w0 = 256 * g + (128 * u if in_order else u)
+                    src = words[:, w0 : w0 + P] if in_order else words[:, w0 : 256 * (g + 1) : 2]
+                    nc.tensor.transpose(tb[:, q, :], src, ident[:])
                 banks.append(tb)
             return banks
 
-        def copy_bank(eng, grp, b, tb):
-            dst = grp[:].bitcast(F32)[:, 512 * b : 512 * (b + 1)].rearrange("p (g r u) -> p g r u", g=2, u=2)
+        def copy_bank(eng, words, b, tb):
+            dst = words[:, 512 * b : 512 * (b + 1)].rearrange("p (g r u) -> p g r u", g=2, u=2)
             src = tb[:].rearrange("p (g u) r -> p g r u", u=2)
             if eng == "s":
                 nc.scalar.copy(out=dst, in_=src)
             else:
                 nc.vector.tensor_copy(out=dst, in_=src)
 
-        def quantise(grp, codes, scl, ng):
-            nc.vector.quantize_mx(
-                out=codes[:, : P * ng].bitcast(FP8X4), scales=scl[:, : P * ng], in_=grp[:, : 512 * ng]
-            )
-
-        hb = transposes(hraw[:].bitcast(F32), 4)
-        hgrp = grpp.tile([P, K], BF16, name="grp", tag="grp", align_bytes=64)
-        copy_bank("s", hgrp, 0, hb[0])
-        copy_bank("v", hgrp, 1, hb[1])
-        xgrp = grpp.tile([P, K], BF16, name="grp", tag="grp", align_bytes=64)
-        nc.vector.tensor_copy(
-            out=xgrp[:].rearrange("p (g c j) -> p g c j", g=4, j=4),
-            in_=xraw[:].rearrange("p a b -> p (a b)").rearrange("p (g j c) -> p g c j", g=4, j=4),
-        )
+        hgrp = const.tile([P, K], BF16, name="hgrp", align_bytes=64)
+        xgrp = const.tile([P, K], BF16, name="xgrp", align_bytes=64)
         act_codes = {}
         act_scales = {}
-        for nm, grp in (("h", hgrp), ("x", xgrp)):
+        bias = {}
+
+        def quantise_act(nm, grp):
             ac = const.tile([P, 512], U32, name="actc_" + nm, align_bytes=64)
             asc = const.tile([P, 512], U8, name="acts_" + nm, align_bytes=64)
-            quantise(grp, ac, asc, 4)
+            nc.vector.quantize_mx(out=ac[:].bitcast(FP8X4), scales=asc[:], in_=grp[:])
             act_codes[nm] = ac
             act_scales[nm] = asc
 
-        bias = {}
-        for gate, n0, n1 in (("i", "ii", "hi"), ("g", "ig", "hg")):
-            bs = const.tile([P, NT], F32, name="bias_" + gate)
-            nc.vector.tensor_tensor(out=bs[:], in0=braw[n0][:], in1=braw[n1][:], op=ALU.add)
-            bias[gate] = bs
+        def transpose_h():
+            hb = transposes(hraw[:].bitcast(F32), 4, False)
+            copy_bank("s", hgrp[:].bitcast(F32), 0, hb[0])
+            copy_bank("v", hgrp[:].bitcast(F32), 1, hb[1])
 
-        unit_codes = {}
+        def group_x():
+            nc.vector.tensor_copy(
+                out=xgrp[:].rearrange("p (g c j) -> p g c j", g=4, j=4),
+                in_=xraw[:].rearrange("p a b -> p (a b)").rearrange("p (g j c) -> p g c j", g=4, j=4),
+            )
 
-        def mx_set(st):
+        def add_biases():
+            for gate, n0, n1 in (("i", "ii", "hi"), ("g", "ig", "hg")):
+                bs = const.tile([P, NT], F32, name="bias_" + gate)
+                nc.vector.tensor_tensor(out=bs[:], in0=braw[n0][:], in1=braw[n1][:], op=ALU.add)
+                bias[gate] = bs
+
+        step_codes = {}
+
+        def mx_run(groups):
             acc = accp.tile([P, 2, B], F32, name="acc", tag="acc")
-            for si, grp in enumerate(st):
+            for si, grp in enumerate(groups):
                 passes = []
                 for ci, j in group_units[grp]:
                     for gl in range(stream[ci][5]):
                         passes.append((ci, j, gl))
                 for pi, (ci, j, gl) in enumerate(passes):
-                    half = stream[ci][1]
-                    g = stream[ci][4] + gl
-                    codes, scl = unit_codes[(ci, j)]
+                    gate, half, t0, n, g0, ng = stream[ci]
+                    g = g0 + gl
+                    c0 = P * (j * ng + gl)
+                    codes, scl = step_codes[ci]
                     nc.tensor.matmul_mx(
                         out=acc[:, si, :],
-                        lhsT=codes[:, P * gl : P * (gl + 1)].bitcast(FP8X4),
-                        lhsT_scale=scl[:, P * gl : P * (gl + 1)],
+                        lhsT=codes[:, c0 : c0 + P].bitcast(FP8X4),
+                        lhsT_scale=scl[:, c0 : c0 + P],
                         rhs=act_codes[half][:, P * g : P * (g + 1)].bitcast(FP8X4),
                         rhs_scale=act_scales[half][:, P * g : P * (g + 1)],
                         start=(pi == 0),
                         stop=(pi == len(passes) - 1),
                     )
-            gate = st[0][0]
-            for si, (gt, t) in enumerate(st):
+            for si, (gate, t) in enumerate(groups):
                 nc.scalar.activation(
                     out=gate_out[gate][:, t, :],
                     in_=acc[:, si, :],
@@ -204,9 +205,9 @@ def tile_naivelstm_pa_kernel(tc, x, h, w_ii, w_ig, w_hi, w_hg, b_ii, b_hi, b_ig,
                     bias=bias[gate][:, t : t + 1],
                     scale=1.0,
                 )
-            hi = st[-1][1] + 1
-            lo = hi - 1 if hi > 2 * PAIRS else hi - 2
-            if gate == "g" and (hi > 2 * PAIRS or hi % 2 == 0):
+            gate, lo = groups[0]
+            hi = groups[-1][1] + 1
+            if gate == "g":
                 nc.vector.tensor_tensor(
                     out=osb[:, lo:hi, :], in0=gate_out["i"][:, lo:hi, :], in1=gate_out["g"][:, lo:hi, :], op=ALU.mult
                 )
@@ -217,52 +218,39 @@ def tile_naivelstm_pa_kernel(tc, x, h, w_ii, w_ig, w_hi, w_hg, b_ii, b_hi, b_ig,
 
         ord_tiles = {}
 
-        def put_in_order(ci, j):
-            ng = stream[ci][5]
-            if ci not in ord_tiles:
+        def put_in_order(ci):
+            if ci < n_steps and ordered[ci]:
+                gate, half, t0, n, g0, ng = stream[ci]
                 ot = ordp.tile([P, 2 * K], BF16, name="ordw", tag="ordw")
+                w = 256 * n * ng
+                nc.vector.tensor_copy(
+                    out=ot[:].bitcast(F32)[:, :w].rearrange("p (g u c) -> p g u c", u=2, c=P),
+                    in_=raw_tiles[ci][:].bitcast(F32)[:, :w].rearrange("p (g c u) -> p g u c", u=2, c=P),
+                )
                 ord_tiles[ci] = ot
-            lo, hi = j * 256 * ng, (j + 1) * 256 * ng
-            nc.vector.tensor_copy(
-                out=ord_tiles[ci][:].bitcast(F32)[:, lo:hi].rearrange("p (g u c) -> p g u c", g=ng, u=2),
-                in_=raw_tiles[ci][:].bitcast(F32)[:, lo:hi].rearrange("p (g c u) -> p g u c", g=ng, u=2),
-            )
-
-        loaded = [NB]
-
-        def next_load():
-            if loaded[0] < n_steps:
-                load(loaded[0])
-                loaded[0] += 1
 
         for ci in range(AHEAD):
-            if ordered[ci]:
-                for j in range(stream[ci][3]):
-                    put_in_order(ci, j)
-        bank_count = 0
+            put_in_order(ci)
         for ci in range(n_steps):
             gate, half, t0, n, g0, ng = stream[ci]
             words = (ord_tiles[ci] if ordered[ci] else raw_tiles[ci])[:].bitcast(F32)
-            banks = []
-            for j in range(n):
-                banks.append(transposes(words[:, j * 256 * ng : (j + 1) * 256 * ng], ng, ordered[ci]))
-            next_load()
-            grps = []
-            for j in range(n):
-                grp = grpp.tile([P, K], BF16, name="grp", tag="grp", align_bytes=64)
-                grps.append(grp)
-                for b, tb in enumerate(banks[j]):
-                    bank_count += 1
-                    copy_bank("v" if (ng == 4 and not ordered[ci] and bank_count % 4 == 0) else "s", grp, b, tb)
-            pre = ci + AHEAD
-            for j in range(n):
-                if pre < n_steps and ordered[pre]:
-                    for jj in range(stream[pre][3]):
-                        if jj % n == j:
-                            put_in_order(pre, jj)
-                codes = codp.tile([P, 512], U32, name="codes", tag="codes", align_bytes=64)
-                scl = codp.tile([P, 512], U8, name="scl", tag="scl", align_bytes=64)
-                quantise(grps[j], codes, scl, ng)
-                unit_codes[(ci, j)] = (codes, scl)
-            for st in runs.get(ci, []):
-                mx_set(st)
+            banks = transposes(words, n * ng, ordered[ci])
+            if ci + NB < n_steps:
+                load(ci + NB)
+            put_in_order(ci + AHEAD)
+            grp = grpp.tile([P, 2 * K], BF16, name="grp", tag="grp", align_bytes=64)
+            for b, tb in enumerate(banks):
+                copy_bank("v" if (b == 1 and len(banks) > 1 and not ordered[ci]) else "s", grp[:].bitcast(F32), b, tb)
+            codes = codp.tile([P, 1024], U32, name="codes", tag="codes", align_bytes=64)
+            scl = codp.tile([P, 1024], U8, name="scl", tag="scl", align_bytes=64)
+            w = P * n * ng
+            nc.vector.quantize_mx(out=codes[:, :w].bitcast(FP8X4), scales=scl[:, :w], in_=grp[:, : 4 * w])
+            step_codes[ci] = (codes, scl)
+            if ci == FIRST - 1:
+                transpose_h()
+                group_x()
+                quantise_act("h", hgrp)
+                quantise_act("x", xgrp)
+                add_biases()
+            for g in runs.get(ci, []):
+                mx_run(g)

@@ -18,7 +18,7 @@ B = 128
 FLOPS = 2 * 4 * 2048 * 2048 * 128
 
 PAIRS = 7
-LAG_PASSES = 16
+LAG_PASSES = 12
 TAIL_STEPS = 4
 NB = 10
 T_BANKS = 6
@@ -78,23 +78,27 @@ def tile_naivelstm_pa_kernel(tc, x, h, w_ii, w_ig, w_hi, w_hg, b_ii, b_hi, b_ig,
             gate, half, t0, n, g0, ng = stream[ci]
             for j in range(n):
                 group_units[(gate, t0 + j)] = group_units.get((gate, t0 + j), []) + [(ci, j)]
-        sets = []
-        for pair in range(PAIRS):
+        order = []
+        for pair in range(NT // 2):
             for gate in "ig":
-                sets.append([(gate, 2 * pair), (gate, 2 * pair + 1)])
+                if pair < PAIRS:
+                    order.append((gate, 2 * pair))
+                    order.append((gate, 2 * pair + 1))
         for gate in "ig":
             for t in range(2 * PAIRS, NT):
-                sets.append([(gate, t)])
+                order.append((gate, t))
         runs = {}
-        for groups in sets:
-            place = group_units[groups[-1]][-1][0]
+        for grp in order:
+            place = group_units[grp][-1][0]
             ahead = 0
             while place < n_steps - 1 and ahead < LAG_PASSES:
                 place += 1
                 ahead += stream[place][3] * stream[place][5]
+            if grp[1] < 2 * PAIRS and grp[1] % 2 == 1:
+                place += 1
             if place >= n_steps - TAIL_STEPS:
                 place = n_steps - 1
-            runs[place] = runs.get(place, []) + [groups]
+            runs[place] = runs.get(place, []) + [grp]
 
         ident = const.tile([P, P], F32, name="ident")
         make_identity(nc, ident[:])
@@ -176,38 +180,37 @@ def tile_naivelstm_pa_kernel(tc, x, h, w_ii, w_ig, w_hi, w_hg, b_ii, b_hi, b_ig,
 
         step_codes = {}
 
-        def mx_run(groups):
-            acc = accp.tile([P, 2, B], F32, name="acc", tag="acc")
-            for si, grp in enumerate(groups):
-                passes = []
-                for ci, j in group_units[grp]:
-                    for gl in range(stream[ci][5]):
-                        passes.append((ci, j, gl))
-                for pi, (ci, j, gl) in enumerate(passes):
-                    gate, half, t0, n, g0, ng = stream[ci]
-                    g = g0 + gl
-                    c0 = P * (j * ng + gl)
-                    codes, scl = step_codes[ci]
-                    nc.tensor.matmul_mx(
-                        out=acc[:, si, :],
-                        lhsT=codes[:, c0 : c0 + P].bitcast(FP8X4),
-                        lhsT_scale=scl[:, c0 : c0 + P],
-                        rhs=act_codes[half][:, P * g : P * (g + 1)].bitcast(FP8X4),
-                        rhs_scale=act_scales[half][:, P * g : P * (g + 1)],
-                        start=(pi == 0),
-                        stop=(pi == len(passes) - 1),
-                    )
-            for si, (gate, t) in enumerate(groups):
-                nc.scalar.activation(
-                    out=gate_out[gate][:, t, :],
-                    in_=acc[:, si, :],
-                    func=(ACT.Sigmoid if gate == "i" else ACT.Tanh),
-                    bias=bias[gate][:, t : t + 1],
-                    scale=1.0,
+        def mx_group(grp):
+            acc = accp.tile([P, B], F32, name="acc", tag="acc")
+            passes = []
+            for ci, j in group_units[grp]:
+                for gl in range(stream[ci][5]):
+                    passes.append((ci, j, gl))
+            for pi, (ci, j, gl) in enumerate(passes):
+                gate, half, t0, n, g0, ng = stream[ci]
+                g = g0 + gl
+                c0 = P * (j * ng + gl)
+                codes, scl = step_codes[ci]
+                nc.tensor.matmul_mx(
+                    out=acc[:],
+                    lhsT=codes[:, c0 : c0 + P].bitcast(FP8X4),
+                    lhsT_scale=scl[:, c0 : c0 + P],
+                    rhs=act_codes[half][:, P * g : P * (g + 1)].bitcast(FP8X4),
+                    rhs_scale=act_scales[half][:, P * g : P * (g + 1)],
+                    start=(pi == 0),
+                    stop=(pi == len(passes) - 1),
                 )
-            gate, lo = groups[0]
-            hi = groups[-1][1] + 1
-            if gate == "g":
+            gate, t = grp
+            nc.scalar.activation(
+                out=gate_out[gate][:, t, :],
+                in_=acc[:],
+                func=(ACT.Sigmoid if gate == "i" else ACT.Tanh),
+                bias=bias[gate][:, t : t + 1],
+                scale=1.0,
+            )
+            hi = t + 1
+            lo = hi - 1 if hi > 2 * PAIRS else hi - 2
+            if gate == "g" and (hi > 2 * PAIRS or hi % 2 == 0):
                 nc.vector.tensor_tensor(
                     out=osb[:, lo:hi, :], in0=gate_out["i"][:, lo:hi, :], in1=gate_out["g"][:, lo:hi, :], op=ALU.mult
                 )
@@ -253,4 +256,4 @@ def tile_naivelstm_pa_kernel(tc, x, h, w_ii, w_ig, w_hi, w_hg, b_ii, b_hi, b_ig,
                 quantise_act("x", xgrp)
                 add_biases()
             for g in runs.get(ci, []):
-                mx_run(g)
+                mx_group(g)

@@ -18,16 +18,16 @@ B = 128
 FLOPS = 2 * 4 * 2048 * 2048 * 128
 
 PAIRS = 7
-LAG_PASSES = 12
-TAIL_STEPS = 4
 NB = 10
 T_BANKS = 6
 ACC_BANKS = 2
-GRP_BUFS = 3
-CODE_BUFS = 7
-ORD_BUFS = 3
+GRP_BUFS = 6
+CODE_BUFS = 14
+ORD_BUFS = 4
 FIRST = 2
-AHEAD = 2
+AHEAD = 3
+MX_LAG = 5
+ACT_AT = 4
 
 
 def tile_naivelstm_pa_kernel(tc, x, h, w_ii, w_ig, w_hi, w_hg, b_ii, b_hi, b_ig, b_hg, out):
@@ -58,7 +58,16 @@ def tile_naivelstm_pa_kernel(tc, x, h, w_ii, w_ig, w_hi, w_hg, b_ii, b_hi, b_ig,
         stream.append(("g", "h", NT - 1, 1, 0, 2))
         stream.append(("g", "h", NT - 1, 1, 2, 2))
         n_steps = len(stream)
-        ordered = [4 <= ci < n_steps - 3 and ci % 2 == 1 for ci in range(n_steps)]
+
+        units = []
+        group_units = {}
+        for ci in range(n_steps):
+            for j in range(stream[ci][3]):
+                grp = (stream[ci][0], stream[ci][2] + j)
+                group_units[grp] = group_units.get(grp, []) + [len(units)]
+                units.append((ci, j))
+        n_units = len(units)
+        ordered = [k % 2 == 1 and 8 <= k < n_units - 3 for k in range(n_units)]
 
         raw_tiles = {}
 
@@ -72,33 +81,6 @@ def tile_naivelstm_pa_kernel(tc, x, h, w_ii, w_ig, w_hi, w_hg, b_ii, b_hi, b_ig,
             else:
                 nc.sync.dma_start(out=rt[:, : n * ng * 512].rearrange("p (t k) -> p t k", t=n), in_=src)
             raw_tiles[ci] = rt
-
-        group_units = {}
-        for ci in range(n_steps):
-            gate, half, t0, n, g0, ng = stream[ci]
-            for j in range(n):
-                group_units[(gate, t0 + j)] = group_units.get((gate, t0 + j), []) + [(ci, j)]
-        order = []
-        for pair in range(NT // 2):
-            for gate in "ig":
-                if pair < PAIRS:
-                    order.append((gate, 2 * pair))
-                    order.append((gate, 2 * pair + 1))
-        for gate in "ig":
-            for t in range(2 * PAIRS, NT):
-                order.append((gate, t))
-        runs = {}
-        for grp in order:
-            place = group_units[grp][-1][0]
-            ahead = 0
-            while place < n_steps - 1 and ahead < LAG_PASSES:
-                place += 1
-                ahead += stream[place][3] * stream[place][5]
-            if grp[1] < 2 * PAIRS and grp[1] % 2 == 1:
-                place += 1
-            if place >= n_steps - TAIL_STEPS:
-                place = n_steps - 1
-            runs[place] = runs.get(place, []) + [grp]
 
         ident = const.tile([P, P], F32, name="ident")
         make_identity(nc, ident[:])
@@ -148,8 +130,6 @@ def tile_naivelstm_pa_kernel(tc, x, h, w_ii, w_ig, w_hi, w_hg, b_ii, b_hi, b_ig,
             else:
                 nc.vector.tensor_copy(out=dst, in_=src)
 
-        hgrp = const.tile([P, K], BF16, name="hgrp", align_bytes=64)
-        xgrp = const.tile([P, K], BF16, name="xgrp", align_bytes=64)
         act_codes = {}
         act_scales = {}
         bias = {}
@@ -161,99 +141,141 @@ def tile_naivelstm_pa_kernel(tc, x, h, w_ii, w_ig, w_hi, w_hg, b_ii, b_hi, b_ig,
             act_codes[nm] = ac
             act_scales[nm] = asc
 
-        def transpose_h():
+        def prepare_activations():
+            hgrp = const.tile([P, K], BF16, name="hgrp", align_bytes=64)
+            xgrp = const.tile([P, K], BF16, name="xgrp", align_bytes=64)
             hb = transposes(hraw[:].bitcast(F32), 4, False)
             copy_bank("s", hgrp[:].bitcast(F32), 0, hb[0])
             copy_bank("v", hgrp[:].bitcast(F32), 1, hb[1])
-
-        def group_x():
             nc.vector.tensor_copy(
                 out=xgrp[:].rearrange("p (g c j) -> p g c j", g=4, j=4),
                 in_=xraw[:].rearrange("p a b -> p (a b)").rearrange("p (g j c) -> p g c j", g=4, j=4),
             )
-
-        def add_biases():
+            quantise_act("h", hgrp)
+            quantise_act("x", xgrp)
             for gate, n0, n1 in (("i", "ii", "hi"), ("g", "ig", "hg")):
                 bs = const.tile([P, NT], F32, name="bias_" + gate)
                 nc.vector.tensor_tensor(out=bs[:], in0=braw[n0][:], in1=braw[n1][:], op=ALU.add)
                 bias[gate] = bs
 
-        step_codes = {}
-
-        def mx_group(grp):
-            acc = accp.tile([P, B], F32, name="acc", tag="acc")
-            passes = []
-            for ci, j in group_units[grp]:
-                for gl in range(stream[ci][5]):
-                    passes.append((ci, j, gl))
-            for pi, (ci, j, gl) in enumerate(passes):
-                gate, half, t0, n, g0, ng = stream[ci]
-                g = g0 + gl
-                c0 = P * (j * ng + gl)
-                codes, scl = step_codes[ci]
-                nc.tensor.matmul_mx(
-                    out=acc[:],
-                    lhsT=codes[:, c0 : c0 + P].bitcast(FP8X4),
-                    lhsT_scale=scl[:, c0 : c0 + P],
-                    rhs=act_codes[half][:, P * g : P * (g + 1)].bitcast(FP8X4),
-                    rhs_scale=act_scales[half][:, P * g : P * (g + 1)],
-                    start=(pi == 0),
-                    stop=(pi == len(passes) - 1),
-                )
-            gate, t = grp
-            nc.scalar.activation(
-                out=gate_out[gate][:, t, :],
-                in_=acc[:],
-                func=(ACT.Sigmoid if gate == "i" else ACT.Tanh),
-                bias=bias[gate][:, t : t + 1],
-                scale=1.0,
-            )
-            hi = t + 1
-            lo = hi - 1 if hi > 2 * PAIRS else hi - 2
-            if gate == "g" and (hi > 2 * PAIRS or hi % 2 == 0):
-                nc.vector.tensor_tensor(
-                    out=osb[:, lo:hi, :], in0=gate_out["i"][:, lo:hi, :], in1=gate_out["g"][:, lo:hi, :], op=ALU.mult
-                )
-                if hi == 2 * PAIRS:
-                    nc.sync.dma_start(out=out_v[:, 0:hi, :], in_=osb[:, 0:hi, :])
-                elif hi > 2 * PAIRS:
-                    nc.sync.dma_start(out=out_v[:, lo:hi, :], in_=osb[:, lo:hi, :])
+        def unit_words(k, tiles):
+            ci, j = units[k]
+            ng = stream[ci][5]
+            return tiles[ci][:].bitcast(F32)[:, 256 * ng * j : 256 * ng * (j + 1)]
 
         ord_tiles = {}
 
-        def put_in_order(ci):
-            if ci < n_steps and ordered[ci]:
-                gate, half, t0, n, g0, ng = stream[ci]
-                ot = ordp.tile([P, 2 * K], BF16, name="ordw", tag="ordw")
-                w = 256 * n * ng
+        def put_in_order(k):
+            if k < n_units and ordered[k]:
+                ng = stream[units[k][0]][5]
+                ot = ordp.tile([P, K], BF16, name="ordw", tag="ordw")
                 nc.vector.tensor_copy(
-                    out=ot[:].bitcast(F32)[:, :w].rearrange("p (g u c) -> p g u c", u=2, c=P),
-                    in_=raw_tiles[ci][:].bitcast(F32)[:, :w].rearrange("p (g c u) -> p g u c", u=2, c=P),
+                    out=ot[:].bitcast(F32)[:, : 256 * ng].rearrange("p (g u c) -> p g u c", u=2, c=P),
+                    in_=unit_words(k, raw_tiles).rearrange("p (g c u) -> p g u c", u=2, c=P),
                 )
-                ord_tiles[ci] = ot
+                ord_tiles[k] = ot
 
-        for ci in range(AHEAD):
-            put_in_order(ci)
-        for ci in range(n_steps):
+        unit_grp = {}
+        unit_codes = {}
+
+        def quantise_unit(k):
+            ng = stream[units[k][0]][5]
+            codes = codp.tile([P, 512], U32, name="codes", tag="codes", align_bytes=64)
+            scl = codp.tile([P, 512], U8, name="scl", tag="scl", align_bytes=64)
+            nc.vector.quantize_mx(
+                out=codes[:, : P * ng].bitcast(FP8X4), scales=scl[:, : P * ng], in_=unit_grp[k][:, : 512 * ng]
+            )
+            unit_codes[k] = (codes, scl)
+
+        accs = {}
+        closed = []
+
+        def mx_unit(k):
+            ci, j = units[k]
             gate, half, t0, n, g0, ng = stream[ci]
-            words = (ord_tiles[ci] if ordered[ci] else raw_tiles[ci])[:].bitcast(F32)
-            banks = transposes(words, n * ng, ordered[ci])
-            if ci + NB < n_steps:
+            grp = (gate, t0 + j)
+            first = k == group_units[grp][0]
+            last = k == group_units[grp][-1]
+            if first:
+                acc = accp.tile([P, B], F32, name="acc", tag="acc")
+                accs[grp] = acc
+            codes, scl = unit_codes[k]
+            for gl in range(ng):
+                g = g0 + gl
+                nc.tensor.matmul_mx(
+                    out=accs[grp][:],
+                    lhsT=codes[:, P * gl : P * (gl + 1)].bitcast(FP8X4),
+                    lhsT_scale=scl[:, P * gl : P * (gl + 1)],
+                    rhs=act_codes[half][:, P * g : P * (g + 1)].bitcast(FP8X4),
+                    rhs_scale=act_scales[half][:, P * g : P * (g + 1)],
+                    start=(first and gl == 0),
+                    stop=(last and gl == ng - 1),
+                )
+            if last:
+                closed.append(grp)
+
+        def finish_closed():
+            while closed:
+                gate, t = closed.pop(0)
+                nc.scalar.activation(
+                    out=gate_out[gate][:, t, :],
+                    in_=accs[(gate, t)][:],
+                    func=(ACT.Sigmoid if gate == "i" else ACT.Tanh),
+                    bias=bias[gate][:, t : t + 1],
+                    scale=1.0,
+                )
+                hi = t + 1
+                lo = hi - 1 if hi > 2 * PAIRS else hi - 2
+                if gate == "g" and (hi > 2 * PAIRS or hi % 2 == 0):
+                    nc.vector.tensor_tensor(
+                        out=osb[:, lo:hi, :], in0=gate_out["i"][:, lo:hi, :], in1=gate_out["g"][:, lo:hi, :], op=ALU.mult
+                    )
+                    if hi == 2 * PAIRS:
+                        nc.sync.dma_start(out=out_v[:, 0:hi, :], in_=osb[:, 0:hi, :])
+                    elif hi > 2 * PAIRS:
+                        nc.sync.dma_start(out=out_v[:, lo:hi, :], in_=osb[:, lo:hi, :])
+
+        mx_order = []
+        for pair in range(NT // 2):
+            for gate in "ig":
+                if pair < PAIRS:
+                    mx_order.append((gate, 2 * pair))
+                    mx_order.append((gate, 2 * pair + 1))
+        for gate in "ig":
+            for t in range(2 * PAIRS, NT):
+                mx_order.append((gate, t))
+
+        for k in range(AHEAD):
+            put_in_order(k)
+        run_after = -2
+        for k in range(n_units):
+            ci, j = units[k]
+            ng = stream[ci][5]
+            if k == ACT_AT:
+                prepare_activations()
+            if ordered[k]:
+                banks = transposes(ord_tiles[k][:].bitcast(F32), ng, True)
+            else:
+                banks = transposes(unit_words(k, raw_tiles), ng, False)
+            if j == stream[ci][3] - 1 and ci + NB < n_steps:
                 load(ci + NB)
-            put_in_order(ci + AHEAD)
-            grp = grpp.tile([P, 2 * K], BF16, name="grp", tag="grp", align_bytes=64)
+            put_in_order(k + AHEAD)
+            grp = grpp.tile([P, K], BF16, name="grp", tag="grp", align_bytes=64)
+            unit_grp[k] = grp
             for b, tb in enumerate(banks):
-                copy_bank("v" if (b == 1 and len(banks) > 1 and not ordered[ci]) else "s", grp[:].bitcast(F32), b, tb)
-            codes = codp.tile([P, 1024], U32, name="codes", tag="codes", align_bytes=64)
-            scl = codp.tile([P, 1024], U8, name="scl", tag="scl", align_bytes=64)
-            w = P * n * ng
-            nc.vector.quantize_mx(out=codes[:, :w].bitcast(FP8X4), scales=scl[:, :w], in_=grp[:, : 4 * w])
-            step_codes[ci] = (codes, scl)
-            if ci == FIRST - 1:
-                transpose_h()
-                group_x()
-                quantise_act("h", hgrp)
-                quantise_act("x", xgrp)
-                add_biases()
-            for g in runs.get(ci, []):
-                mx_group(g)
+                on_vector = b == 1 and ng == 4 and (k % 4 == 0)
+                copy_bank("v" if on_vector else "s", grp[:].bitcast(F32), b, tb)
+            if k >= 1:
+                quantise_unit(k - 1)
+            finish_closed()
+            if mx_order and group_units[mx_order[0]][-1] <= k - MX_LAG and k >= run_after + 2:
+                for u in group_units[mx_order.pop(0)]:
+                    mx_unit(u)
+                run_after = k
+        for k in range(n_units - 1, n_units):
+            quantise_unit(k)
+        finish_closed()
+        while mx_order:
+            for u in group_units[mx_order.pop(0)]:
+                mx_unit(u)
+            finish_closed()

from contextlib import ExitStack

import concourse.mybir as mybir
from concourse.masks import make_identity

F32 = mybir.dt.float32
BF16 = mybir.dt.bfloat16
U32 = mybir.dt.uint32
U8 = mybir.dt.uint8
FP8X4 = mybir.dt.float8_e4m3fn_x4
ACT = mybir.ActivationFunctionType
ALU = mybir.AluOpType

P = 128
K = 2048
NT = 16
B = 128
FLOPS = 2 * 4 * 2048 * 2048 * 128

PAIRS = 7
NB = 10
T_BANKS = 6
ACC_BANKS = 2
GRP_BUFS = 6
CODE_BUFS = 14
ORD_BUFS = 4
FIRST = 2
AHEAD = 3
MX_LAG = 5
ACT_AT = 4


def tile_naivelstm_pa_kernel(tc, x, h, w_ii, w_ig, w_hi, w_hg, b_ii, b_hi, b_ig, b_hg, out):
    nc = tc.nc
    with ExitStack() as ctx:
        ctx.enter_context(tc.manual_schedule())
        const = ctx.enter_context(tc.tile_pool(name="const", bufs=1))
        rawp = ctx.enter_context(tc.tile_pool(name="rawp", bufs=NB))
        ordp = ctx.enter_context(tc.tile_pool(name="ordp", bufs=ORD_BUFS))
        grpp = ctx.enter_context(tc.tile_pool(name="grpp", bufs=GRP_BUFS))
        codp = ctx.enter_context(tc.tile_pool(name="codp", bufs=CODE_BUFS))
        tps = ctx.enter_context(tc.psum_pool(name="tps", bufs=T_BANKS))
        accp = ctx.enter_context(tc.psum_pool(name="accp", bufs=ACC_BANKS))

        weights = {("i", "x"): w_ii, ("i", "h"): w_hi, ("g", "x"): w_ig, ("g", "h"): w_hg}
        out_v = out.rearrange("(p t) b -> p t b", t=NT)

        stream = []
        for pair in range(PAIRS):
            for gate in "ig":
                for half in "xh":
                    stream.append((gate, half, 2 * pair, 2, 0, 4))
        for gate in "ig":
            for t in range(2 * PAIRS, NT):
                for half in "xh":
                    stream.append((gate, half, t, 1, 0, 4))
        stream.pop()
        stream.append(("g", "h", NT - 1, 1, 0, 2))
        stream.append(("g", "h", NT - 1, 1, 2, 2))
        n_steps = len(stream)

        units = []
        group_units = {}
        for ci in range(n_steps):
            for j in range(stream[ci][3]):
                grp = (stream[ci][0], stream[ci][2] + j)
                group_units[grp] = group_units.get(grp, []) + [len(units)]
                units.append((ci, j))
        n_units = len(units)
        ordered = [k % 2 == 1 and 8 <= k < n_units - 3 for k in range(n_units)]

        raw_tiles = {}

        def load(ci):
            gate, half, t0, n, g0, ng = stream[ci]
            rt = rawp.tile([P, 2 * K], BF16, name="wraw", tag="wraw")
            src = weights[(gate, half)].rearrange("(p t) k -> p t k", t=NT)[:, t0 : t0 + n, 512 * g0 : 512 * (g0 + ng)]
            if ci == 0:
                for j in range(n):
                    nc.sync.dma_start(out=rt[:, j * K : (j + 1) * K], in_=src[:, j, :])
            else:
                nc.sync.dma_start(out=rt[:, : n * ng * 512].rearrange("p (t k) -> p t k", t=n), in_=src)
            raw_tiles[ci] = rt

        ident = const.tile([P, P], F32, name="ident")
        make_identity(nc, ident[:])

        braw = {}
        for nm, ap in (("ii", b_ii), ("hi", b_hi), ("ig", b_ig), ("hg", b_hg)):
            bt = const.tile([P, NT], BF16, name="braw_" + nm)
            nc.scalar.dma_start(out=bt[:], in_=ap.rearrange("(p t) o -> p (t o)", t=NT))
            braw[nm] = bt

        for ci in range(FIRST):
            load(ci)
        hraw = const.tile([P, K], BF16, name="hraw")
        nc.sync.dma_start(out=hraw[:], in_=h)
        xraw = const.tile([P, 4, 512], BF16, name="xraw")
        nc.sync.dma_start(out=xraw[:], in_=x.rearrange("(g p t) c -> p g (t c)", g=4, p=P, t=4))
        for ci in range(FIRST, NB):
            load(ci)

        warm = const.tile([P, 1], F32, name="warm")
        nc.vector.memset(warm[:], 0.0)
        warm2 = const.tile([P, 1], F32, name="warm2")
        nc.scalar.activation(out=warm2[:], in_=warm[:], func=ACT.Sigmoid)

        gate_out = {}
        for gate in "ig":
            gate_out[gate] = const.tile([P, NT, B], F32, name="gate_" + gate)
        osb = const.tile([P, NT, B], F32, name="osb")

        def transposes(words, ng, in_order):
            banks = []
            for b in range(ng // 2):
                tb = tps.tile([P, 4, P], F32, name="tb", tag="tb")
                for q in range(4):
                    g, u = 2 * b + q // 2, q % 2
                    w0 = 256 * g + (128 * u if in_order else u)
                    src = words[:, w0 : w0 + P] if in_order else words[:, w0 : 256 * (g + 1) : 2]
                    nc.tensor.transpose(tb[:, q, :], src, ident[:])
                banks.append(tb)
            return banks

        def copy_bank(eng, words, b, tb):
            dst = words[:, 512 * b : 512 * (b + 1)].rearrange("p (g r u) -> p g r u", g=2, u=2)
            src = tb[:].rearrange("p (g u) r -> p g r u", u=2)
            if eng == "s":
                nc.scalar.copy(out=dst, in_=src)
            else:
                nc.vector.tensor_copy(out=dst, in_=src)

        act_codes = {}
        act_scales = {}
        bias = {}

        def quantise_act(nm, grp):
            ac = const.tile([P, 512], U32, name="actc_" + nm, align_bytes=64)
            asc = const.tile([P, 512], U8, name="acts_" + nm, align_bytes=64)
            nc.vector.quantize_mx(out=ac[:].bitcast(FP8X4), scales=asc[:], in_=grp[:])
            act_codes[nm] = ac
            act_scales[nm] = asc

        def prepare_activations():
            hgrp = const.tile([P, K], BF16, name="hgrp", align_bytes=64)
            xgrp = const.tile([P, K], BF16, name="xgrp", align_bytes=64)
            hb = transposes(hraw[:].bitcast(F32), 4, False)
            copy_bank("s", hgrp[:].bitcast(F32), 0, hb[0])
            copy_bank("v", hgrp[:].bitcast(F32), 1, hb[1])
            nc.vector.tensor_copy(
                out=xgrp[:].rearrange("p (g c j) -> p g c j", g=4, j=4),
                in_=xraw[:].rearrange("p a b -> p (a b)").rearrange("p (g j c) -> p g c j", g=4, j=4),
            )
            quantise_act("h", hgrp)
            quantise_act("x", xgrp)
            for gate, n0, n1 in (("i", "ii", "hi"), ("g", "ig", "hg")):
                bs = const.tile([P, NT], F32, name="bias_" + gate)
                nc.vector.tensor_tensor(out=bs[:], in0=braw[n0][:], in1=braw[n1][:], op=ALU.add)
                bias[gate] = bs

        def unit_words(k, tiles):
            ci, j = units[k]
            ng = stream[ci][5]
            return tiles[ci][:].bitcast(F32)[:, 256 * ng * j : 256 * ng * (j + 1)]

        ord_tiles = {}

        def put_in_order(k):
            if k < n_units and ordered[k]:
                ng = stream[units[k][0]][5]
                ot = ordp.tile([P, K], BF16, name="ordw", tag="ordw")
                nc.vector.tensor_copy(
                    out=ot[:].bitcast(F32)[:, : 256 * ng].rearrange("p (g u c) -> p g u c", u=2, c=P),
                    in_=unit_words(k, raw_tiles).rearrange("p (g c u) -> p g u c", u=2, c=P),
                )
                ord_tiles[k] = ot

        unit_grp = {}
        unit_codes = {}

        def quantise_unit(k):
            ng = stream[units[k][0]][5]
            codes = codp.tile([P, 512], U32, name="codes", tag="codes", align_bytes=64)
            scl = codp.tile([P, 512], U8, name="scl", tag="scl", align_bytes=64)
            nc.vector.quantize_mx(
                out=codes[:, : P * ng].bitcast(FP8X4), scales=scl[:, : P * ng], in_=unit_grp[k][:, : 512 * ng]
            )
            unit_codes[k] = (codes, scl)

        accs = {}
        closed = []

        def mx_unit(k):
            ci, j = units[k]
            gate, half, t0, n, g0, ng = stream[ci]
            grp = (gate, t0 + j)
            first = k == group_units[grp][0]
            last = k == group_units[grp][-1]
            if first:
                acc = accp.tile([P, B], F32, name="acc", tag="acc")
                accs[grp] = acc
            codes, scl = unit_codes[k]
            for gl in range(ng):
                g = g0 + gl
                nc.tensor.matmul_mx(
                    out=accs[grp][:],
                    lhsT=codes[:, P * gl : P * (gl + 1)].bitcast(FP8X4),
                    lhsT_scale=scl[:, P * gl : P * (gl + 1)],
                    rhs=act_codes[half][:, P * g : P * (g + 1)].bitcast(FP8X4),
                    rhs_scale=act_scales[half][:, P * g : P * (g + 1)],
                    start=(first and gl == 0),
                    stop=(last and gl == ng - 1),
                )
            if last:
                closed.append(grp)

        def finish_closed():
            while closed:
                gate, t = closed.pop(0)
                nc.scalar.activation(
                    out=gate_out[gate][:, t, :],
                    in_=accs[(gate, t)][:],
                    func=(ACT.Sigmoid if gate == "i" else ACT.Tanh),
                    bias=bias[gate][:, t : t + 1],
                    scale=1.0,
                )
                hi = t + 1
                lo = hi - 1 if hi > 2 * PAIRS else hi - 2
                if gate == "g" and (hi > 2 * PAIRS or hi % 2 == 0):
                    nc.vector.tensor_tensor(
                        out=osb[:, lo:hi, :], in0=gate_out["i"][:, lo:hi, :], in1=gate_out["g"][:, lo:hi, :], op=ALU.mult
                    )
                    if hi == 2 * PAIRS:
                        nc.sync.dma_start(out=out_v[:, 0:hi, :], in_=osb[:, 0:hi, :])
                    elif hi > 2 * PAIRS:
                        nc.sync.dma_start(out=out_v[:, lo:hi, :], in_=osb[:, lo:hi, :])

        mx_order = []
        for pair in range(NT // 2):
            for gate in "ig":
                if pair < PAIRS:
                    mx_order.append((gate, 2 * pair))
                    mx_order.append((gate, 2 * pair + 1))
        for gate in "ig":
            for t in range(2 * PAIRS, NT):
                mx_order.append((gate, t))

        for k in range(AHEAD):
            put_in_order(k)
        run_after = -2
        for k in range(n_units):
            ci, j = units[k]
            ng = stream[ci][5]
            if k == ACT_AT:
                prepare_activations()
            if ordered[k]:
                banks = transposes(ord_tiles[k][:].bitcast(F32), ng, True)
            else:
                banks = transposes(unit_words(k, raw_tiles), ng, False)
            if j == stream[ci][3] - 1 and ci + NB < n_steps:
                load(ci + NB)
            put_in_order(k + AHEAD)
            grp = grpp.tile([P, K], BF16, name="grp", tag="grp", align_bytes=64)
            unit_grp[k] = grp
            for b, tb in enumerate(banks):
                on_vector = b == 1 and ng == 4 and (k % 4 == 0)
                copy_bank("v" if on_vector else "s", grp[:].bitcast(F32), b, tb)
            if k >= 1:
                quantise_unit(k - 1)
            finish_closed()
            if mx_order and group_units[mx_order[0]][-1] <= k - MX_LAG and k >= run_after + 2:
                for u in group_units[mx_order.pop(0)]:
                    mx_unit(u)
                run_after = k
        for k in range(n_units - 1, n_units):
            quantise_unit(k)
        finish_closed()
        while mx_order:
            for u in group_units[mx_order.pop(0)]:
                mx_unit(u)
            finish_closed()
